import numpy as np
import ml_dtypes


def mxq(x, axis, fmt="e4m3"):
    dtype, down = {"e4m3": (ml_dtypes.float8_e4m3fn, 7), "e5m2": (ml_dtypes.float8_e5m2, 14)}[fmt]
    v = np.moveaxis(np.asarray(x, np.float32).astype(ml_dtypes.bfloat16).astype(np.float64), axis, -1)
    blocks = v.reshape(v.shape[:-1] + (-1, 32))
    amax = np.abs(blocks).max(-1, keepdims=True)
    byte = np.maximum(np.where(amax > 0, np.frexp(amax)[1] - 1 + 127, 0) - down, 1)
    scale = np.exp2(byte - 127.0)
    codes = (blocks / scale).astype(np.float32).astype(dtype).astype(np.float64)
    return np.moveaxis((codes * scale).reshape(v.shape), -1, axis)


WIDE = False


def mx_kscale(k):
    if not WIDE:
        return np.ones(k)
    levels = np.array([10, -10, 5, -5, 0])
    if k % 512:
        return np.exp2(np.random.permutation(np.resize(levels, k // 32))).repeat(32)
    a = np.empty((k // 512, 16))
    for p in range(k // 512):
        a[p, :8] = np.random.permutation(np.resize(levels, 8))
        for g in range(8):
            far = levels[np.abs(levels - a[p, g]) >= 10]
            a[p, g + 8] = far[np.random.randint(len(far))]
    return np.exp2(a.ravel()).repeat(32)


BF16 = ml_dtypes.bfloat16


def bf(x):
    return np.asarray(x, np.float32).astype(BF16)


def f64(x):
    return np.asarray(x).astype(np.float64)


B, T, D, E, F = 4, 1024, 512, 1024, 256
EPS = 1e-6


def rms_norm(x, w):
    rms = np.sqrt(np.mean(x * x, axis=-1, keepdims=True) + EPS)
    return x / rms * w


def erf(v):
    a = np.minimum(np.abs(v), 6.0)
    z = 2.0 * a * a
    term = a.copy()
    tot = a.copy()
    for n in range(1, 110):
        term = term * z / (2 * n + 1)
        tot = tot + term
    return np.sign(v) * tot * np.exp(-a * a) * 2.0 / np.sqrt(np.pi)


def gelu_erf(v):
    return 0.5 * v * (1.0 + erf(v / np.sqrt(2.0)))


def draw0():
    s, t = mx_kscale(E), mx_kscale(D)
    return {"attn": bf(np.random.standard_normal((B, T, E)) * 0.6 * s),
            "x": bf(np.random.standard_normal((B, T, D))),
            "wo": bf(np.random.standard_normal((E, D)) / np.sqrt(E) / s[:, None]),
            "bo": bf(np.random.standard_normal(D) * 0.1),
            "mlp_norm_w": bf((1.0 + 0.1 * np.random.standard_normal(D)) * t),
            "w1": bf(np.random.standard_normal((D, F)) / np.sqrt(D) / t[:, None]),
            "b1": bf(np.random.standard_normal(F) * 0.1)}


def core(attn, x, wo, bo, mlp_norm_w, w1, b1):
    x_mid = f64(x) + (mxq(f64(attn), 2, "e4m3") @ mxq(f64(wo), 0, "e4m3")) + f64(bo)
    h = rms_norm(x_mid, f64(mlp_norm_w))
    g = gelu_erf((mxq(h, 2, "e4m3") @ mxq(f64(w1), 0, "e4m3")) + f64(b1))
    return x_mid, g


def e4m3fn_bytes(y):
    return np.clip(np.asarray(y, np.float64), -448.0, 448.0).astype(np.float32).astype(ml_dtypes.float8_e4m3fn).view(np.uint8)


def e4m3fn_values(b):
    return np.asarray(b, np.uint8).view(ml_dtypes.float8_e4m3fn).astype(np.float64)


def setup_inputs():
    d = draw0()
    x0 = np.asarray(d['attn']).astype(np.float64)
    s = (np.max(np.abs(x0), axis=(0, 1), keepdims=True) / 448.0).astype(np.float32)
    out = {}
    for k, v in d.items():
        if k == 'attn':
            out['attn_bytes'] = e4m3fn_bytes(x0 / s.astype(np.float64))
            out['attn_scale'] = s
        else:
            out[k] = v
    return out


def reference(attn_bytes, attn_scale, x, wo, bo, mlp_norm_w, w1, b1):
    return core(e4m3fn_values(attn_bytes) * attn_scale.astype(np.float64), x, wo, bo, mlp_norm_w, w1, b1)

@@ -1,0 +1,249 @@
+from contextlib import ExitStack
+
+import concourse.mybir as mybir
+from concourse.masks import make_identity
+
+TOK, E, D, F = 4096, 1024, 512, 256
+EPS = 1e-6
+FLOPS = 2 * TOK * E * D + 2 * TOK * D * F
+
+F32 = mybir.dt.float32
+BF16 = mybir.dt.bfloat16
+U32 = mybir.dt.uint32
+U8 = mybir.dt.uint8
+FP8 = mybir.dt.float8_e4m3fn
+FP8X4 = mybir.dt.float8_e4m3fn_x4
+ALU = mybir.AluOpType
+ACT = mybir.ActivationFunctionType
+
+P = 128
+J = 4
+G = TOK // (P * J)
+N_TILES = G * J
+
+
+def tile_tinyblock_pb_t_kernel(tc, attn_bytes, attn_scale, x, wo, bo, mlp_norm_w, w1, b1, out_0, out_1):
+    nc = tc.nc
+    bytes_view = attn_bytes.rearrange("b (g p j) k -> (b g) p j k", p=P, j=J)
+    x_view = x.rearrange("b (g p j) d -> (b g) p j d", p=P, j=J)
+    out0_view = out_0.rearrange("b (g p j) d -> (b g) p j d", p=P, j=J)
+    out1_view = out_1.rearrange("b (g p j) f -> (b g) p j f", p=P, j=J)
+    wo_view = wo.rearrange("(g p t) n -> g p t n", p=P, t=4)
+
+    with ExitStack() as ctx:
+        keep = ctx.enter_context(tc.tile_pool(name="keep", bufs=1))
+        loads = ctx.enter_context(tc.tile_pool(name="loads", bufs=G))
+        work = ctx.enter_context(tc.tile_pool(name="work", bufs=3))
+        work4 = ctx.enter_context(tc.tile_pool(name="work4", bufs=4))
+        work2 = ctx.enter_context(tc.tile_pool(name="work2", bufs=2))
+        ps2 = ctx.enter_context(tc.psum_pool(name="ps2", bufs=2))
+        ps1 = ctx.enter_context(tc.psum_pool(name="ps1", bufs=1))
+        ctx.enter_context(tc.manual_schedule())
+
+        sc_sb = keep.tile([P, 8], F32, name="sc_sb")
+        w_sb = keep.tile([P, 4], BF16, name="w_sb")
+        b1_raw = keep.tile([P, 2], BF16, name="b1_raw")
+        b1_sb = keep.tile([P, 2], F32, name="b1_sb")
+        bo_row = keep.tile([P, D], BF16, name="bo_row")
+        bo_sb = keep.tile([P, D], F32, name="bo_sb")
+        ones = keep.tile([P, P], BF16, name="ones")
+        ident = keep.tile([P, P], F32, name="ident")
+        neg_half = keep.tile([P, 2], F32, name="neg_half")
+        wo_raw = [keep.tile([P, 4, D], BF16, name="wo_raw%d" % g) for g in range(2)]
+        wo_grp = [keep.tile([P, D * 4], BF16, name="wo_grp%d" % g, align_bytes=64) for g in range(2)]
+        wo_codes = [keep.tile([P, D], U32, name="wo_codes%d" % g, align_bytes=64) for g in range(2)]
+        wo_scales = [keep.tile([P, D], U8, name="wo_scales%d" % g, align_bytes=64) for g in range(2)]
+        w1_raw = keep.tile([P, 4, F], BF16, name="w1_raw")
+        w1_grp = keep.tile([P, F * 4], BF16, name="w1_grp", align_bytes=64)
+        w1_codes = keep.tile([P, F], U32, name="w1_codes", align_bytes=64)
+        w1_scales = keep.tile([P, F], U8, name="w1_scales", align_bytes=64)
+        a_bytes = [loads.tile([P, J, E], U8, name="a_bytes") for g in range(G)]
+        x_sb = [loads.tile([P, J, D], BF16, name="x_sb") for g in range(G)]
+
+        nc.vector.memset(bo_row[:], 0.0)
+        nc.scalar.dma_start(out=sc_sb[:].rearrange("p (g t) -> p g t", g=2), in_=attn_scale.rearrange("a b (g p t) -> p (a b g) t", p=P, t=4))
+        nc.scalar.dma_start(out=w_sb[:], in_=mlp_norm_w.rearrange("(p t) -> p t", t=4))
+        nc.scalar.dma_start(out=b1_raw[:], in_=b1.rearrange("(p i) -> p i", i=2))
+        nc.scalar.dma_start(out=bo_row[0:1, :], in_=bo.rearrange("(a d) -> a d", a=1))
+        nc.sync.dma_start(out=a_bytes[0][:, 0:2, :], in_=bytes_view[0][:, 0:2, :])
+        nc.sync.dma_start(out=wo_raw[1][:], in_=wo_view[1])
+        nc.sync.dma_start(out=wo_raw[0][:], in_=wo_view[0])
+        nc.sync.dma_start(out=x_sb[0][:], in_=x_view[0])
+        nc.sync.dma_start(out=a_bytes[0][:, 2:4, :], in_=bytes_view[0][:, 2:4, :])
+        nc.sync.dma_start(out=w1_raw[:], in_=w1.rearrange("(p t) f -> p t f", t=4))
+        for g in range(1, G):
+            nc.sync.dma_start(out=a_bytes[g][:], in_=bytes_view[g])
+            nc.sync.dma_start(out=x_sb[g][:], in_=x_view[g])
+
+        make_identity(nc, ident[:])
+        nc.gpsimd.memset(ones[:], 1.0)
+        nc.gpsimd.memset(neg_half[:], -0.5)
+
+        wide, psa, grp, codes, scales, psm, xbo, xmid, ss, hs, psh, hgrp, hq, hqs, psg, gl, pso, og = ({} for n in range(18))
+        scale4 = sc_sb[:].rearrange("p (g u e) -> p g u e", g=2, u=2)
+
+        def widen(i):
+            g, j = divmod(i, J)
+            wide[i] = work.tile([P, E], BF16, name="wide")
+            nc.scalar.copy(out=wide[i][:], in_=a_bytes[g][:, j, :].bitcast(FP8))
+
+        def t_attn(i):
+            psa[i] = ps2.tile([P, 4, P], F32, name="psa")
+            words = wide[i][:].bitcast(F32)
+            for g in range(2):
+                for u in range(2):
+                    nc.tensor.transpose(psa[i][:, 2 * g + u, :], words[:, 256 * g + u : 256 * (g + 1) : 2], ident[:])
+
+        def prod(i):
+            grp[i] = work.tile([P, 2 * 512], BF16, name="grp", align_bytes=64)
+            for g in range(2):
+                nc.vector.tensor_tensor(
+                    out=grp[i][:, 512 * g : 512 * (g + 1)].rearrange("p (r u e) -> p r u e", u=2, e=2),
+                    in0=psa[i][:, 2 * g : 2 * g + 2, :].bitcast(BF16).rearrange("p u (r e) -> p r u e", e=2),
+                    in1=scale4[:, g, :, :].unsqueeze(1).to_broadcast([P, P, 2, 2]),
+                    op=ALU.mult,
+                )
+
+        def q_attn(i):
+            codes[i] = work.tile([P, 2 * P], U32, name="codes", align_bytes=64)
+            scales[i] = work.tile([P, 2 * P], U8, name="scales", align_bytes=64)
+            nc.vector.quantize_mx(out=codes[i][:].bitcast(FP8X4), scales=scales[i][:], in_=grp[i][:])
+
+        def mx1(i):
+            psm[i] = ps2.tile([P, D], F32, name="psm")
+            for g in range(2):
+                cols = slice(P * g, P * (g + 1))
+                nc.tensor.matmul_mx(out=psm[i][:], lhsT=codes[i][:, cols].bitcast(FP8X4), lhsT_scale=scales[i][:, cols],
+                                    rhs=wo_codes[g][:].bitcast(FP8X4), rhs_scale=wo_scales[g][:], start=(g == 0), stop=(g == 1))
+
+        def x_bias(m):
+            g, h = divmod(m, 2)
+            xbo[m] = work.tile([P, 2, D], F32, name="xbo")
+            nc.gpsimd.tensor_tensor(out=xbo[m][:], in0=x_sb[g][:, 2 * h : 2 * h + 2, :], in1=bo_sb[:].unsqueeze(1).to_broadcast([P, 2, D]), op=ALU.add)
+
+        def add(i):
+            if i % 2 == 0:
+                xmid[i // 2] = work4.tile([P, 2, D], F32, name="xmid")
+            nc.vector.tensor_tensor(out=xmid[i // 2][:, i % 2, :], in0=psm[i][:], in1=xbo[i // 2][:, i % 2, :], op=ALU.add)
+            if i % 2 == 1:
+                g, j = divmod(i, J)
+                nc.sync.dma_start(out=out0_view[g][:, j - 1 : j + 1, :], in_=xmid[i // 2][:])
+
+        def square(i):
+            junk = work2.tile([P, D], BF16, name="junk")
+            if i % 2 == 0:
+                ss[i // 2] = work4.tile([P, 2], F32, name="ss")
+            nc.scalar.activation(out=junk[:], in_=xmid[i // 2][:, i % 2, :], func=ACT.Square, accum_out=ss[i // 2][:, i % 2 : i % 2 + 1])
+
+        def norm(m):
+            ms = work4.tile([P, 2], F32, name="ms")
+            rstd = work4.tile([P, 2], F32, name="rstd")
+            nc.gpsimd.tensor_scalar(out=ms[:], in0=ss[m][:], scalar1=1.0 / D, scalar2=EPS, op0=ALU.mult, op1=ALU.add)
+            nc.gpsimd.tensor_tensor(out=rstd[:], in0=ms[:], in1=neg_half[:], op=ALU.pow)
+            for h in range(2):
+                hs[2 * m + h] = work4.tile([P, D], F32, name="hs")
+                nc.gpsimd.tensor_scalar(out=hs[2 * m + h][:], in0=xmid[m][:, h, :], scalar1=rstd[:, h : h + 1], scalar2=1.0, op0=ALU.mult, op1=ALU.mult)
+
+        def t_hs(i):
+            psh[i] = ps2.tile([P, 4, P], F32, name="psh")
+            for t in range(4):
+                nc.tensor.transpose(psh[i][:, t, :], hs[i][:, t : D : 4], ident[:])
+
+        def gain(i):
+            m, h = divmod(i, 2)
+            if h == 0:
+                hgrp[m] = work2.tile([P, 2 * D], BF16, name="hgrp", align_bytes=64)
+            nc.vector.tensor_tensor(
+                out=hgrp[m][:, D * h : D * (h + 1)].rearrange("p (r t) -> p r t", t=4),
+                in0=psh[i][:].rearrange("p t r -> p r t"),
+                in1=w_sb[:].unsqueeze(1).to_broadcast([P, P, 4]),
+                op=ALU.mult,
+            )
+
+        def q_h(m):
+            hq[m] = work2.tile([P, 2 * P], U32, name="hq", align_bytes=64)
+            hqs[m] = work2.tile([P, 2 * P], U8, name="hqs", align_bytes=64)
+            nc.vector.quantize_mx(out=hq[m][:].bitcast(FP8X4), scales=hqs[m][:], in_=hgrp[m][:])
+
+        def mx2(m):
+            psg[m] = ps1.tile([P, 2, 2 * P], F32, name="psg")
+            for i in range(2):
+                cols = slice(P * i, P * (i + 1))
+                nc.tensor.matmul_mx(out=psg[m][:, i, :], lhsT=w1_codes[:, cols].bitcast(FP8X4), lhsT_scale=w1_scales[:, cols],
+                                    rhs=hq[m][:].bitcast(FP8X4), rhs_scale=hqs[m][:], start=True, stop=True)
+
+        def gelu(m):
+            gl[m] = work2.tile([P, 2, 2 * P], F32, name="gl")
+            for i in range(2):
+                nc.scalar.activation(out=gl[m][:, i, :], in_=psg[m][:, i, :], func=ACT.Gelu, bias=b1_sb[:, i : i + 1], scale=1.0)
+
+        def t_out(m):
+            pso[m] = ps1.tile([P, 2, 2, P], F32, name="pso")
+            for j in range(2):
+                for i in range(2):
+                    nc.tensor.transpose(pso[m][:, j, i, :], gl[m][:, i, P * j : P * (j + 1)], ident[:])
+
+        def copy_out(m):
+            g, h = divmod(m, 2)
+            og[m] = work2.tile([P, 2, F], F32, name="og")
+            nc.scalar.copy(out=og[m][:].rearrange("p j (m i) -> p j m i", i=2), in_=pso[m][:].rearrange("p j i m -> p j m i"))
+            nc.sync.dma_start(out=out1_view[g][:, 2 * h : 2 * h + 2, :], in_=og[m][:])
+
+        def in_range(i, n=N_TILES):
+            return 0 <= i < n
+
+        widen(0)
+        t_attn(0)
+        psb = ps2.tile([P, D], F32, name="psm")
+        nc.tensor.matmul(psb[:], lhsT=ones[:], rhs=bo_row[:], start=True, stop=True)
+        nc.scalar.copy(out=bo_sb[:], in_=psb[:])
+        widen(1)
+        nc.vector.tensor_copy(out=b1_sb[:], in_=b1_raw[:])
+        nc.gpsimd.tensor_scalar(out=wo_grp[1][:].rearrange("p (n t) -> p n t", t=4), in0=wo_raw[1][:].rearrange("p t n -> p n t"),
+                                scalar1=1.0, scalar2=0.0, op0=ALU.mult, op1=ALU.add)
+        x_bias(0)
+        pairs = N_TILES // 2
+
+        for s in range(N_TILES + 9):
+            even = s % 2 == 0
+            if even and in_range(s // 2 + 1, pairs):
+                x_bias(s // 2 + 1)
+            if not even and in_range((s - 3) // 2, pairs):
+                norm((s - 3) // 2)
+            if s == 2:
+                nc.gpsimd.tensor_scalar(out=w1_grp[:].rearrange("p (i m t) -> p i m t", i=2, t=4), in0=w1_raw[:].rearrange("p t (m i) -> p i m t", i=2),
+                                        scalar1=1.0, scalar2=0.0, op0=ALU.mult, op1=ALU.add)
+            if in_range(s + 1):
+                t_attn(s + 1)
+            if in_range(s - 4):
+                t_hs(s - 4)
+            if not even and in_range((s - 9) // 2, pairs):
+                t_out((s - 9) // 2)
+            if in_range(s):
+                prod(s)
+            if s == 0:
+                nc.vector.tensor_copy(out=wo_grp[0][:].rearrange("p (n t) -> p n t", t=4), in_=wo_raw[0][:].rearrange("p t n -> p n t"))
+                for g in (1, 0):
+                    nc.vector.quantize_mx(out=wo_codes[g][:].bitcast(FP8X4), scales=wo_scales[g][:], in_=wo_grp[g][:])
+            if s == 4:
+                nc.vector.quantize_mx(out=w1_codes[:].bitcast(FP8X4), scales=w1_scales[:], in_=w1_grp[:])
+            if not even and in_range((s - 7) // 2, pairs):
+                q_h((s - 7) // 2)
+            if in_range(s - 1):
+                add(s - 1)
+            if in_range(s):
+                q_attn(s)
+            if in_range(s - 5):
+                gain(s - 5)
+            if in_range(s + 2):
+                widen(s + 2)
+            if even and in_range((s - 8) // 2, pairs):
+                gelu((s - 8) // 2)
+            if not even and in_range((s - 9) // 2, pairs):
+                copy_out((s - 9) // 2)
+            if in_range(s):
+                mx1(s)
+            if not even and in_range((s - 7) // 2, pairs):
+                mx2((s - 7) // 2)
+            if in_range(s - 1):
+                square(s - 1)

@@ -34,6 +34,7 @@ def tile_tinyblock_pb_t_kernel(tc, attn_bytes, attn_scale, x, wo, bo, mlp_norm_w
         keep = ctx.enter_context(tc.tile_pool(name="keep", bufs=1))
         loads = ctx.enter_context(tc.tile_pool(name="loads", bufs=G))
         work = ctx.enter_context(tc.tile_pool(name="work", bufs=3))
+        work6 = ctx.enter_context(tc.tile_pool(name="work6", bufs=6))
         work4 = ctx.enter_context(tc.tile_pool(name="work4", bufs=4))
         work2 = ctx.enter_context(tc.tile_pool(name="work2", bufs=2))
         ps2 = ctx.enter_context(tc.psum_pool(name="ps2", bufs=2))
@@ -79,12 +80,12 @@ def tile_tinyblock_pb_t_kernel(tc, attn_bytes, attn_scale, x, wo, bo, mlp_norm_w
         nc.gpsimd.memset(ones[:], 1.0)
         nc.gpsimd.memset(neg_half[:], -0.5)
 
-        wide, psa, grp, codes, scales, psm, xbo, xmid, ss, hs, psh, hgrp, hq, hqs, psg, gl, pso, og = ({} for n in range(18))
+        wide, psa, grp, codes, scales, psm, xbo, xmid, ss, hs, psh, hgrp, hq, hqs, psg, gl, pso, og, rstd = ({} for n in range(19))
         scale4 = sc_sb[:].rearrange("p (g u e) -> p g u e", g=2, u=2)
 
         def widen(i):
             g, j = divmod(i, J)
-            wide[i] = work.tile([P, E], BF16, name="wide")
+            wide[i] = work6.tile([P, E], BF16, name="wide")
             nc.scalar.copy(out=wide[i][:], in_=a_bytes[g][:, j, :].bitcast(FP8))
 
         def t_attn(i):
@@ -95,25 +96,33 @@ def tile_tinyblock_pb_t_kernel(tc, attn_bytes, attn_scale, x, wo, bo, mlp_norm_w
                     nc.tensor.transpose(psa[i][:, 2 * g + u, :], words[:, 256 * g + u : 256 * (g + 1) : 2], ident[:])
 
         def prod(i):
-            grp[i] = work.tile([P, 2 * 512], BF16, name="grp", align_bytes=64)
+            m, h = divmod(i, 2)
+            if h == 0:
+                grp[m] = work2.tile([P, 4 * 512], BF16, name="grp", align_bytes=64)
             for g in range(2):
+                c0 = 512 * (2 * h + g)
                 nc.vector.tensor_tensor(
-                    out=grp[i][:, 512 * g : 512 * (g + 1)].rearrange("p (r u e) -> p r u e", u=2, e=2),
+                    out=grp[m][:, c0 : c0 + 512].rearrange("p (r u e) -> p r u e", u=2, e=2),
                     in0=psa[i][:, 2 * g : 2 * g + 2, :].bitcast(BF16).rearrange("p u (r e) -> p r u e", e=2),
                     in1=scale4[:, g, :, :].unsqueeze(1).to_broadcast([P, P, 2, 2]),
                     op=ALU.mult,
                 )
 
-        def q_attn(i):
-            codes[i] = work.tile([P, 2 * P], U32, name="codes", align_bytes=64)
-            scales[i] = work.tile([P, 2 * P], U8, name="scales", align_bytes=64)
-            nc.vector.quantize_mx(out=codes[i][:].bitcast(FP8X4), scales=scales[i][:], in_=grp[i][:])
+        def q_attn(m):
+            codes[m] = work.tile([P, 4 * P], U32, name="codes", align_bytes=64)
+            scales[m] = work.tile([P, 4 * P], U8, name="scales", align_bytes=64)
+            nc.vector.quantize_mx(out=codes[m][:].bitcast(FP8X4), scales=scales[m][:], in_=grp[m][:])
+
+        def token(m):
+            mark = work2.tile([P, 1], U32, name="mark")
+            nc.gpsimd.tensor_copy(out=mark[:], in_=codes[m][:, 0:1])
 
         def mx1(i):
+            m, h = divmod(i, 2)
             psm[i] = ps2.tile([P, D], F32, name="psm")
             for g in range(2):
-                cols = slice(P * g, P * (g + 1))
-                nc.tensor.matmul_mx(out=psm[i][:], lhsT=codes[i][:, cols].bitcast(FP8X4), lhsT_scale=scales[i][:, cols],
+                cols = slice(P * (2 * h + g), P * (2 * h + g + 1))
+                nc.tensor.matmul_mx(out=psm[i][:], lhsT=codes[m][:, cols].bitcast(FP8X4), lhsT_scale=scales[m][:, cols],
                                     rhs=wo_codes[g][:].bitcast(FP8X4), rhs_scale=wo_scales[g][:], start=(g == 0), stop=(g == 1))
 
         def x_bias(m):
@@ -137,17 +146,26 @@ def tile_tinyblock_pb_t_kernel(tc, attn_bytes, attn_scale, x, wo, bo, mlp_norm_w
 
         def norm(m):
             ms = work4.tile([P, 2], F32, name="ms")
-            rstd = work4.tile([P, 2], F32, name="rstd")
+            rstd[m] = work4.tile([P, 2], F32, name="rstd")
             nc.gpsimd.tensor_scalar(out=ms[:], in0=ss[m][:], scalar1=1.0 / D, scalar2=EPS, op0=ALU.mult, op1=ALU.add)
-            nc.gpsimd.tensor_tensor(out=rstd[:], in0=ms[:], in1=neg_half[:], op=ALU.pow)
-            for h in range(2):
-                hs[2 * m + h] = work4.tile([P, D], F32, name="hs")
-                nc.gpsimd.tensor_scalar(out=hs[2 * m + h][:], in0=xmid[m][:, h, :], scalar1=rstd[:, h : h + 1], scalar2=1.0, op0=ALU.mult, op1=ALU.mult)
+            nc.gpsimd.tensor_tensor(out=rstd[m][:], in0=ms[:], in1=neg_half[:], op=ALU.pow)
+
+        def hs_scale(i, engine):
+            m, h = divmod(i, 2)
+            hs[i] = work4.tile([P, 4, P], F32, name="hs")
+            src = xmid[m][:, h, :].rearrange("p (q t) -> p t q", t=4)
+            r = rstd[m][:, h : h + 1]
+            if engine == "scalar":
+                nc.scalar.activation(out=hs[i][:], in_=src, func=ACT.Copy, scale=r)
+            elif engine == "vector":
+                nc.vector.tensor_scalar(out=hs[i][:], in0=src, scalar1=r, scalar2=None, op0=ALU.mult)
+            else:
+                nc.gpsimd.tensor_scalar(out=hs[i][:], in0=src, scalar1=r, scalar2=1.0, op0=ALU.mult, op1=ALU.mult)
 
         def t_hs(i):
             psh[i] = ps2.tile([P, 4, P], F32, name="psh")
             for t in range(4):
-                nc.tensor.transpose(psh[i][:, t, :], hs[i][:, t : D : 4], ident[:])
+                nc.tensor.transpose(psh[i][:, t, :], hs[i][:, t, :], ident[:])
 
         def gain(i):
             m, h = divmod(i, 2)
@@ -203,47 +221,66 @@ def tile_tinyblock_pb_t_kernel(tc, attn_bytes, attn_scale, x, wo, bo, mlp_norm_w
                                 scalar1=1.0, scalar2=0.0, op0=ALU.mult, op1=ALU.add)
         x_bias(0)
         pairs = N_TILES // 2
+        widen(2)
+        t_attn(1)
+        widen(3)
 
-        for s in range(N_TILES + 9):
-            even = s % 2 == 0
-            if even and in_range(s // 2 + 1, pairs):
-                x_bias(s // 2 + 1)
-            if not even and in_range((s - 3) // 2, pairs):
-                norm((s - 3) // 2)
-            if s == 2:
-                nc.gpsimd.tensor_scalar(out=w1_grp[:].rearrange("p (i m t) -> p i m t", i=2, t=4), in0=w1_raw[:].rearrange("p t (m i) -> p i m t", i=2),
-                                        scalar1=1.0, scalar2=0.0, op0=ALU.mult, op1=ALU.add)
-            if in_range(s + 1):
-                t_attn(s + 1)
-            if in_range(s - 4):
-                t_hs(s - 4)
-            if not even and in_range((s - 9) // 2, pairs):
-                t_out((s - 9) // 2)
-            if in_range(s):
-                prod(s)
+        for s in range(pairs + 4):
+            if in_range(s - 4, pairs):
+                gelu(s - 4)
+            if in_range(s, pairs):
+                prod(2 * s)
             if s == 0:
                 nc.vector.tensor_copy(out=wo_grp[0][:].rearrange("p (n t) -> p n t", t=4), in_=wo_raw[0][:].rearrange("p t n -> p n t"))
-                for g in (1, 0):
-                    nc.vector.quantize_mx(out=wo_codes[g][:].bitcast(FP8X4), scales=wo_scales[g][:], in_=wo_grp[g][:])
-            if s == 4:
-                nc.vector.quantize_mx(out=w1_codes[:].bitcast(FP8X4), scales=w1_scales[:], in_=w1_grp[:])
-            if not even and in_range((s - 7) // 2, pairs):
-                q_h((s - 7) // 2)
-            if in_range(s - 1):
-                add(s - 1)
-            if in_range(s):
+            if in_range(s, pairs):
+                prod(2 * s + 1)
+            if in_range(s - 2, pairs):
+                t_hs(2 * s - 4)
+            if in_range(s + 1, pairs):
+                t_attn(2 * s + 2)
+            if in_range(s - 2, pairs):
+                t_hs(2 * s - 3)
+            if in_range(s + 1, pairs):
+                t_attn(2 * s + 3)
+            if in_range(s - 4, pairs):
+                t_out(s - 4)
+            if in_range(s - 1, pairs):
+                add(2 * s - 2)
+                add(2 * s - 1)
+            if in_range(s - 3, pairs):
+                q_h(s - 3)
+            if in_range(s, pairs):
                 q_attn(s)
-            if in_range(s - 5):
-                gain(s - 5)
-            if in_range(s + 2):
-                widen(s + 2)
-            if even and in_range((s - 8) // 2, pairs):
-                gelu((s - 8) // 2)
-            if not even and in_range((s - 9) // 2, pairs):
-                copy_out((s - 9) // 2)
-            if in_range(s):
-                mx1(s)
-            if not even and in_range((s - 7) // 2, pairs):
-                mx2((s - 7) // 2)
-            if in_range(s - 1):
-                square(s - 1)
+            if s == 0:
+                for g in (0, 1):
+                    nc.vector.quantize_mx(out=wo_codes[g][:].bitcast(FP8X4), scales=wo_scales[g][:], in_=wo_grp[g][:])
+            if s == 2:
+                nc.vector.quantize_mx(out=w1_codes[:].bitcast(FP8X4), scales=w1_scales[:], in_=w1_grp[:])
+            if in_range(s - 2, pairs):
+                gain(2 * s - 4)
+                gain(2 * s - 3)
+            if in_range(s, pairs):
+                mx1(2 * s)
+                mx1(2 * s + 1)
+            if in_range(s - 3, pairs):
+                mx2(s - 3)
+            if in_range(s + 2, pairs):
+                widen(2 * s + 4)
+            if in_range(s - 1, pairs):
+                square(2 * s - 2)
+                square(2 * s - 1)
+            if in_range(s + 2, pairs):
+                widen(2 * s + 5)
+            if in_range(s, pairs):
+                token(s)
+            if s == 1:
+                nc.gpsimd.tensor_scalar(out=w1_grp[:].rearrange("p (i m t) -> p i m t", i=2, t=4), in0=w1_raw[:].rearrange("p t (m i) -> p i m t", i=2),
+                                        scalar1=1.0, scalar2=0.0, op0=ALU.mult, op1=ALU.add)
+            if in_range(s - 1, pairs):
+                norm(s - 1)
+                hs_scale(2 * s - 2, "vector" if s == pairs else "gpsimd")
+                hs_scale(2 * s - 1, "scalar")
+            if in_range(s + 1, pairs):
+                x_bias(s + 1)
+            if in_range(s - 4, pairs):
+                copy_out(s - 4)

@@ -38,11 +38,14 @@ def tile_tinyblock_pb_t_kernel(tc, attn_bytes, attn_scale, x, wo, bo, mlp_norm_w
         work4 = ctx.enter_context(tc.tile_pool(name="work4", bufs=4))
         work2 = ctx.enter_context(tc.tile_pool(name="work2", bufs=2))
         ps2 = ctx.enter_context(tc.psum_pool(name="ps2", bufs=2))
+        psh_pool = ctx.enter_context(tc.psum_pool(name="psh_pool", bufs=1))
+        psa_pool = ctx.enter_context(tc.psum_pool(name="psa_pool", bufs=3))
         ps1 = ctx.enter_context(tc.psum_pool(name="ps1", bufs=1))
         ctx.enter_context(tc.manual_schedule())
 
         sc_sb = keep.tile([P, 8], F32, name="sc_sb")
-        w_sb = keep.tile([P, 4], BF16, name="w_sb")
+        w_row = keep.tile([P, D], BF16, name="w_row")
+        w_bc = keep.tile([P, D], F32, name="w_bc")
         b1_raw = keep.tile([P, 2], BF16, name="b1_raw")
         b1_sb = keep.tile([P, 2], F32, name="b1_sb")
         bo_row = keep.tile([P, D], BF16, name="bo_row")
@@ -62,15 +65,16 @@ def tile_tinyblock_pb_t_kernel(tc, attn_bytes, attn_scale, x, wo, bo, mlp_norm_w
         x_sb = [loads.tile([P, J, D], BF16, name="x_sb") for g in range(G)]
 
         nc.vector.memset(bo_row[:], 0.0)
+        nc.vector.memset(w_row[:], 0.0)
         nc.scalar.dma_start(out=sc_sb[:].rearrange("p (g t) -> p g t", g=2), in_=attn_scale.rearrange("a b (g p t) -> p (a b g) t", p=P, t=4))
-        nc.scalar.dma_start(out=w_sb[:], in_=mlp_norm_w.rearrange("(p t) -> p t", t=4))
+        nc.scalar.dma_start(out=w_row[0:1, :], in_=mlp_norm_w.rearrange("(a d) -> a d", a=1))
         nc.scalar.dma_start(out=b1_raw[:], in_=b1.rearrange("(p i) -> p i", i=2))
         nc.scalar.dma_start(out=bo_row[0:1, :], in_=bo.rearrange("(a d) -> a d", a=1))
         nc.sync.dma_start(out=a_bytes[0][:, 0:2, :], in_=bytes_view[0][:, 0:2, :])
-        nc.sync.dma_start(out=wo_raw[1][:], in_=wo_view[1])
         nc.sync.dma_start(out=wo_raw[0][:], in_=wo_view[0])
-        nc.sync.dma_start(out=x_sb[0][:], in_=x_view[0])
         nc.sync.dma_start(out=a_bytes[0][:, 2:4, :], in_=bytes_view[0][:, 2:4, :])
+        nc.sync.dma_start(out=wo_raw[1][:], in_=wo_view[1])
+        nc.sync.dma_start(out=x_sb[0][:], in_=x_view[0])
         nc.sync.dma_start(out=w1_raw[:], in_=w1.rearrange("(p t) f -> p t f", t=4))
         for g in range(1, G):
             nc.sync.dma_start(out=a_bytes[g][:], in_=bytes_view[g])
@@ -80,7 +84,7 @@ def tile_tinyblock_pb_t_kernel(tc, attn_bytes, attn_scale, x, wo, bo, mlp_norm_w
         nc.gpsimd.memset(ones[:], 1.0)
         nc.gpsimd.memset(neg_half[:], -0.5)
 
-        wide, psa, grp, codes, scales, psm, xbo, xmid, ss, hs, psh, hgrp, hq, hqs, psg, gl, pso, og, rstd = ({} for n in range(19))
+        wide, psa, grp, codes, scales, psm, xbo, xmid, ss, hs, psh, hgrp, hq, hqs, psg, gl, pso, og, rstd, mean = ({} for n in range(20))
         scale4 = sc_sb[:].rearrange("p (g u e) -> p g u e", g=2, u=2)
 
         def widen(i):
@@ -89,7 +93,7 @@ def tile_tinyblock_pb_t_kernel(tc, attn_bytes, attn_scale, x, wo, bo, mlp_norm_w
             nc.scalar.copy(out=wide[i][:], in_=a_bytes[g][:, j, :].bitcast(FP8))
 
         def t_attn(i):
-            psa[i] = ps2.tile([P, 4, P], F32, name="psa")
+            psa[i] = psa_pool.tile([P, 4, P], F32, name="psa")
             words = wide[i][:].bitcast(F32)
             for g in range(2):
                 for u in range(2):
@@ -114,8 +118,12 @@ def tile_tinyblock_pb_t_kernel(tc, attn_bytes, attn_scale, x, wo, bo, mlp_norm_w
             nc.vector.quantize_mx(out=codes[m][:].bitcast(FP8X4), scales=scales[m][:], in_=grp[m][:])
 
         def token(m):
-            mark = work2.tile([P, 1], U32, name="mark")
-            nc.gpsimd.tensor_copy(out=mark[:], in_=codes[m][:, 0:1])
+            if m < 2:
+                mark = work2.tile([P, 1], U32, name="mark")
+                nc.gpsimd.tensor_copy(out=mark[:], in_=codes[m][:, 0:1])
+            else:
+                markh = work2.tile([P, 1], BF16, name="markh")
+                nc.gpsimd.tensor_copy(out=markh[:], in_=hs[2 * m - 3][:, 0:1])
 
         def mx1(i):
             m, h = divmod(i, 2)
@@ -144,106 +152,100 @@ def tile_tinyblock_pb_t_kernel(tc, attn_bytes, attn_scale, x, wo, bo, mlp_norm_w
                 ss[i // 2] = work4.tile([P, 2], F32, name="ss")
             nc.scalar.activation(out=junk[:], in_=xmid[i // 2][:, i % 2, :], func=ACT.Square, accum_out=ss[i // 2][:, i % 2 : i % 2 + 1])
 
-        def norm(m):
-            ms = work4.tile([P, 2], F32, name="ms")
-            rstd[m] = work4.tile([P, 2], F32, name="rstd")
-            nc.gpsimd.tensor_scalar(out=ms[:], in0=ss[m][:], scalar1=1.0 / D, scalar2=EPS, op0=ALU.mult, op1=ALU.add)
-            nc.gpsimd.tensor_tensor(out=rstd[m][:], in0=ms[:], in1=neg_half[:], op=ALU.pow)
-
-        def hs_scale(i, engine):
-            m, h = divmod(i, 2)
-            hs[i] = work4.tile([P, 4, P], F32, name="hs")
-            src = xmid[m][:, h, :].rearrange("p (q t) -> p t q", t=4)
-            r = rstd[m][:, h : h + 1]
-            if engine == "scalar":
-                nc.scalar.activation(out=hs[i][:], in_=src, func=ACT.Copy, scale=r)
-            elif engine == "vector":
-                nc.vector.tensor_scalar(out=hs[i][:], in0=src, scalar1=r, scalar2=None, op0=ALU.mult)
-            else:
-                nc.gpsimd.tensor_scalar(out=hs[i][:], in0=src, scalar1=r, scalar2=1.0, op0=ALU.mult, op1=ALU.mult)
-
-        def t_hs(i):
-            psh[i] = ps2.tile([P, 4, P], F32, name="psh")
-            for t in range(4):
-                nc.tensor.transpose(psh[i][:, t, :], hs[i][:, t, :], ident[:])
+        def norm(m, a=0, b=2):
+            if a == 0:
+                rstd[m] = work4.tile([P, 2], F32, name="rstd")
+                mean[m] = work4.tile([P, 2], F32, name="mean")
+            nc.gpsimd.tensor_scalar(out=mean[m][:, a:b], in0=ss[m][:, a:b], scalar1=1.0 / D, scalar2=EPS, op0=ALU.mult, op1=ALU.add)
+            nc.gpsimd.tensor_tensor(out=rstd[m][:, a:b], in0=mean[m][:, a:b], in1=neg_half[:, a:b], op=ALU.pow)
 
         def gain(i):
             m, h = divmod(i, 2)
+            hs[i] = work4.tile([P, D], BF16, name="hs")
+            nc.vector.scalar_tensor_tensor(out=hs[i][:], in0=xmid[m][:, h, :], scalar=rstd[m][:, h : h + 1], in1=w_bc[:], op0=ALU.mult, op1=ALU.mult)
+
+        def t_h(i):
+            m, h = divmod(i, 2)
             if h == 0:
+                psh[m] = psh_pool.tile([P, 2, 2, P], F32, name="psh")
+            words = hs[i][:].bitcast(F32)
+            for u in range(2):
+                nc.tensor.transpose(psh[m][:, h, u, :], words[:, u : D // 2 : 2], ident[:])
+
+        def h_copy(m, a=0, b=2, engine=nc.scalar.copy):
+            if a == 0:
                 hgrp[m] = work2.tile([P, 2 * D], BF16, name="hgrp", align_bytes=64)
-            nc.vector.tensor_tensor(
-                out=hgrp[m][:, D * h : D * (h + 1)].rearrange("p (r t) -> p r t", t=4),
-                in0=psh[i][:].rearrange("p t r -> p r t"),
-                in1=w_sb[:].unsqueeze(1).to_broadcast([P, P, 4]),
-                op=ALU.mult,
-            )
+            engine(out=hgrp[m][:, D * a : D * b].bitcast(F32).rearrange("p (h r u) -> p h r u", h=b - a, u=2), in_=psh[m][:, a:b, :, :].rearrange("p h u r -> p h r u"))
 
-        def q_h(m):
-            hq[m] = work2.tile([P, 2 * P], U32, name="hq", align_bytes=64)
-            hqs[m] = work2.tile([P, 2 * P], U8, name="hqs", align_bytes=64)
-            nc.vector.quantize_mx(out=hq[m][:].bitcast(FP8X4), scales=hqs[m][:], in_=hgrp[m][:])
+        def q_h(m, a=0, b=2):
+            if a == 0:
+                hq[m] = work2.tile([P, 2 * P], U32, name="hq", align_bytes=64)
+                hqs[m] = work2.tile([P, 2 * P], U8, name="hqs", align_bytes=64)
+            nc.vector.quantize_mx(out=hq[m][:, P * a : P * b].bitcast(FP8X4), scales=hqs[m][:, P * a : P * b], in_=hgrp[m][:, D * a : D * b])
 
-        def mx2(m):
-            psg[m] = ps1.tile([P, 2, 2 * P], F32, name="psg")
+        def mx2(m, a=0, b=2, pool=ps1, name="psg"):
+            psg[m, a] = pool.tile([P, 2, P * (b - a)], F32, name=name)
             for i in range(2):
                 cols = slice(P * i, P * (i + 1))
-                nc.tensor.matmul_mx(out=psg[m][:, i, :], lhsT=w1_codes[:, cols].bitcast(FP8X4), lhsT_scale=w1_scales[:, cols],
-                                    rhs=hq[m][:].bitcast(FP8X4), rhs_scale=hqs[m][:], start=True, stop=True)
+                nc.tensor.matmul_mx(out=psg[m, a][:, i, :], lhsT=w1_codes[:, cols].bitcast(FP8X4), lhsT_scale=w1_scales[:, cols],
+                                    rhs=hq[m][:, P * a : P * b].bitcast(FP8X4), rhs_scale=hqs[m][:, P * a : P * b], start=True, stop=True)
 
-        def gelu(m):
-            gl[m] = work2.tile([P, 2, 2 * P], F32, name="gl")
+        def gelu(m, a=0, b=2):
+            gl[m, a] = work4.tile([P, 2, P * (b - a)], F32, name="gl")
             for i in range(2):
-                nc.scalar.activation(out=gl[m][:, i, :], in_=psg[m][:, i, :], func=ACT.Gelu, bias=b1_sb[:, i : i + 1], scale=1.0)
+                nc.scalar.activation(out=gl[m, a][:, i, :], in_=psg[m, a][:, i, :], func=ACT.Gelu, bias=b1_sb[:, i : i + 1], scale=1.0)
 
-        def t_out(m):
-            pso[m] = ps1.tile([P, 2, 2, P], F32, name="pso")
-            for j in range(2):
+        def t_out(m, a=0, b=2, pool=ps1, name="pso"):
+            pso[m, a] = pool.tile([P, b - a, 2, P], F32, name=name)
+            for j in range(b - a):
                 for i in range(2):
-                    nc.tensor.transpose(pso[m][:, j, i, :], gl[m][:, i, P * j : P * (j + 1)], ident[:])
+                    nc.tensor.transpose(pso[m, a][:, j, i, :], gl[m, a][:, i, P * j : P * (j + 1)], ident[:])
 
-        def copy_out(m):
+        def copy_out(m, a=0, b=2, engine=nc.scalar.copy):
             g, h = divmod(m, 2)
-            og[m] = work2.tile([P, 2, F], F32, name="og")
-            nc.scalar.copy(out=og[m][:].rearrange("p j (m i) -> p j m i", i=2), in_=pso[m][:].rearrange("p j i m -> p j m i"))
-            nc.sync.dma_start(out=out1_view[g][:, 2 * h : 2 * h + 2, :], in_=og[m][:])
+            og[m, a] = work4.tile([P, b - a, F], F32, name="og")
+            engine(out=og[m, a][:].rearrange("p j (m i) -> p j m i", i=2), in_=pso[m, a][:].rearrange("p j i m -> p j m i"))
+            nc.sync.dma_start(out=out1_view[g][:, 2 * h + a : 2 * h + b, :], in_=og[m, a][:])
 
         def in_range(i, n=N_TILES):
             return 0 <= i < n
 
+        pairs = N_TILES // 2
         widen(0)
         t_attn(0)
+        widen(1)
+        t_attn(1)
         psb = ps2.tile([P, D], F32, name="psm")
         nc.tensor.matmul(psb[:], lhsT=ones[:], rhs=bo_row[:], start=True, stop=True)
+        widen(2)
+        widen(3)
         nc.scalar.copy(out=bo_sb[:], in_=psb[:])
-        widen(1)
-        nc.vector.tensor_copy(out=b1_sb[:], in_=b1_raw[:])
+        psw = ps2.tile([P, D], F32, name="psm")
+        nc.tensor.matmul(psw[:], lhsT=ones[:], rhs=w_row[:], start=True, stop=True)
+        nc.scalar.copy(out=w_bc[:], in_=psw[:])
+        nc.vector.tensor_copy(out=wo_grp[0][:].rearrange("p (n t) -> p n t", t=4), in_=wo_raw[0][:].rearrange("p t n -> p n t"))
         nc.gpsimd.tensor_scalar(out=wo_grp[1][:].rearrange("p (n t) -> p n t", t=4), in0=wo_raw[1][:].rearrange("p t n -> p n t"),
                                 scalar1=1.0, scalar2=0.0, op0=ALU.mult, op1=ALU.add)
         x_bias(0)
-        pairs = N_TILES // 2
-        widen(2)
-        t_attn(1)
-        widen(3)
 
-        for s in range(pairs + 4):
+        for s in range(pairs):
             if in_range(s - 4, pairs):
                 gelu(s - 4)
             if in_range(s, pairs):
                 prod(2 * s)
-            if s == 0:
-                nc.vector.tensor_copy(out=wo_grp[0][:].rearrange("p (n t) -> p n t", t=4), in_=wo_raw[0][:].rearrange("p t n -> p n t"))
-            if in_range(s, pairs):
-                prod(2 * s + 1)
-            if in_range(s - 2, pairs):
-                t_hs(2 * s - 4)
+            if in_range(s - 3, pairs):
+                t_h(2 * s - 6)
+                t_h(2 * s - 5)
             if in_range(s + 1, pairs):
                 t_attn(2 * s + 2)
-            if in_range(s - 2, pairs):
-                t_hs(2 * s - 3)
+            if in_range(s, pairs):
+                prod(2 * s + 1)
             if in_range(s + 1, pairs):
                 t_attn(2 * s + 3)
             if in_range(s - 4, pairs):
                 t_out(s - 4)
+            if in_range(s - 3, pairs):
+                h_copy(s - 3)
             if in_range(s - 1, pairs):
                 add(2 * s - 2)
                 add(2 * s - 1)
@@ -254,6 +256,8 @@ def tile_tinyblock_pb_t_kernel(tc, attn_bytes, attn_scale, x, wo, bo, mlp_norm_w
             if s == 0:
                 for g in (0, 1):
                     nc.vector.quantize_mx(out=wo_codes[g][:].bitcast(FP8X4), scales=wo_scales[g][:], in_=wo_grp[g][:])
+            if s == 1:
+                nc.vector.tensor_copy(out=b1_sb[:], in_=b1_raw[:])
             if s == 2:
                 nc.vector.quantize_mx(out=w1_codes[:].bitcast(FP8X4), scales=w1_scales[:], in_=w1_grp[:])
             if in_range(s - 2, pairs):
@@ -278,9 +282,51 @@ def tile_tinyblock_pb_t_kernel(tc, attn_bytes, attn_scale, x, wo, bo, mlp_norm_w
                                         scalar1=1.0, scalar2=0.0, op0=ALU.mult, op1=ALU.add)
             if in_range(s - 1, pairs):
                 norm(s - 1)
-                hs_scale(2 * s - 2, "vector" if s == pairs else "gpsimd")
-                hs_scale(2 * s - 1, "scalar")
             if in_range(s + 1, pairs):
                 x_bias(s + 1)
             if in_range(s - 4, pairs):
                 copy_out(s - 4)
+        last = pairs - 1
+        t_h(2 * last - 4)
+        t_h(2 * last - 3)
+        add(2 * last)
+        square(2 * last)
+        add(2 * last + 1)
+        norm(last, 0, 1)
+        gelu(last - 3)
+        square(2 * last + 1)
+        h_copy(last - 2)
+        gain(2 * last - 2)
+        gain(2 * last - 1)
+        q_h(last - 2)
+        gain(2 * last)
+        norm(last, 1, 2)
+        t_out(last - 3)
+        t_h(2 * last - 2)
+        t_h(2 * last - 1)
+        mx2(last - 2)
+        h_copy(last - 1)
+        t_h(2 * last)
+        gain(2 * last + 1)
+        copy_out(last - 3)
+        q_h(last - 1)
+        t_h(2 * last + 1)
+        gelu(last - 2)
+        h_copy(last, 0, 1, nc.vector.tensor_copy)
+        mx2(last - 1)
+        q_h(last, 0, 1)
+        t_out(last - 2)
+        h_copy(last, 1, 2, nc.vector.tensor_copy)
+        mx2(last, 0, 1, ps2, "psm")
+        q_h(last, 1, 2)
+        gelu(last - 1)
+        mx2(last, 1, 2, ps2, "psm")
+        copy_out(last - 2, 0, 2, nc.vector.tensor_copy)
+        gelu(last, 0, 1)
+        t_out(last - 1)
+        gelu(last, 1, 2)
+        t_out(last, 0, 1, psa_pool, "psa")
+        copy_out(last - 1, 0, 2, nc.vector.tensor_copy)
+        t_out(last, 1, 2, psa_pool, "psa")
+        copy_out(last, 0, 1)
+        copy_out(last, 1, 2, nc.vector.tensor_copy)

@@ -117,17 +117,14 @@ def tile_tinyblock_pb_t_kernel(tc, attn_bytes, attn_scale, x, wo, bo, mlp_norm_w
             scales[m] = work.tile([P, 4 * P], U8, name="scales", align_bytes=64)
             nc.vector.quantize_mx(out=codes[m][:].bitcast(FP8X4), scales=scales[m][:], in_=grp[m][:])
 
-        def token(m):
-            if m < 2:
-                mark = work2.tile([P, 1], U32, name="mark")
-                nc.gpsimd.tensor_copy(out=mark[:], in_=codes[m][:, 0:1])
-            else:
-                markh = work2.tile([P, 1], BF16, name="markh")
-                nc.gpsimd.tensor_copy(out=markh[:], in_=hs[2 * m - 3][:, 0:1])
+        def filler(i):
+            psm[i] = ps2.tile([P, D], F32, name="psm")
+            nc.tensor.matmul(psm[i][:], lhsT=ones[:], rhs=bo_row[:], start=True, stop=True)
 
         def mx1(i):
             m, h = divmod(i, 2)
-            psm[i] = ps2.tile([P, D], F32, name="psm")
+            if i not in psm:
+                psm[i] = ps2.tile([P, D], F32, name="psm")
             for g in range(2):
                 cols = slice(P * (2 * h + g), P * (2 * h + g + 1))
                 nc.tensor.matmul_mx(out=psm[i][:], lhsT=codes[m][:, cols].bitcast(FP8X4), lhsT_scale=scales[m][:, cols],
@@ -156,7 +153,7 @@ def tile_tinyblock_pb_t_kernel(tc, attn_bytes, attn_scale, x, wo, bo, mlp_norm_w
             if a == 0:
                 rstd[m] = work4.tile([P, 2], F32, name="rstd")
                 mean[m] = work4.tile([P, 2], F32, name="mean")
-            nc.gpsimd.tensor_scalar(out=mean[m][:, a:b], in0=ss[m][:, a:b], scalar1=1.0 / D, scalar2=EPS, op0=ALU.mult, op1=ALU.add)
+            nc.vector.tensor_scalar(out=mean[m][:, a:b], in0=ss[m][:, a:b], scalar1=1.0 / D, scalar2=EPS, op0=ALU.mult, op1=ALU.add)
             nc.gpsimd.tensor_tensor(out=rstd[m][:, a:b], in0=mean[m][:, a:b], in1=neg_half[:, a:b], op=ALU.pow)
 
         def gain(i):
@@ -229,30 +226,32 @@ def tile_tinyblock_pb_t_kernel(tc, attn_bytes, attn_scale, x, wo, bo, mlp_norm_w
         x_bias(0)
 
         for s in range(pairs):
-            if in_range(s - 4, pairs):
-                gelu(s - 4)
-            if in_range(s, pairs):
-                prod(2 * s)
+            if in_range(s - 5, pairs):
+                gelu(s - 5)
+            prod(2 * s)
             if in_range(s - 3, pairs):
                 t_h(2 * s - 6)
                 t_h(2 * s - 5)
             if in_range(s + 1, pairs):
                 t_attn(2 * s + 2)
-            if in_range(s, pairs):
-                prod(2 * s + 1)
+            if in_range(s - 1, pairs):
+                mx1(2 * s - 1)
+            prod(2 * s + 1)
             if in_range(s + 1, pairs):
                 t_attn(2 * s + 3)
-            if in_range(s - 4, pairs):
-                t_out(s - 4)
+            if in_range(s - 5, pairs):
+                t_out(s - 5)
             if in_range(s - 3, pairs):
                 h_copy(s - 3)
+            if in_range(s - 4, pairs):
+                mx2(s - 4)
             if in_range(s - 1, pairs):
                 add(2 * s - 2)
+                filler(2 * s)
                 add(2 * s - 1)
             if in_range(s - 3, pairs):
                 q_h(s - 3)
-            if in_range(s, pairs):
-                q_attn(s)
+            q_attn(s)
             if s == 0:
                 for g in (0, 1):
                     nc.vector.quantize_mx(out=wo_codes[g][:].bitcast(FP8X4), scales=wo_scales[g][:], in_=wo_grp[g][:])
@@ -263,11 +262,9 @@ def tile_tinyblock_pb_t_kernel(tc, attn_bytes, attn_scale, x, wo, bo, mlp_norm_w
             if in_range(s - 2, pairs):
                 gain(2 * s - 4)
                 gain(2 * s - 3)
-            if in_range(s, pairs):
-                mx1(2 * s)
-                mx1(2 * s + 1)
-            if in_range(s - 3, pairs):
-                mx2(s - 3)
+            mx1(2 * s)
+            if s < 14:
+                filler(2 * s + 1)
             if in_range(s + 2, pairs):
                 widen(2 * s + 4)
             if in_range(s - 1, pairs):
@@ -275,8 +272,6 @@ def tile_tinyblock_pb_t_kernel(tc, attn_bytes, attn_scale, x, wo, bo, mlp_norm_w
                 square(2 * s - 1)
             if in_range(s + 2, pairs):
                 widen(2 * s + 5)
-            if in_range(s, pairs):
-                token(s)
             if s == 1:
                 nc.gpsimd.tensor_scalar(out=w1_grp[:].rearrange("p (i m t) -> p i m t", i=2, t=4), in0=w1_raw[:].rearrange("p t (m i) -> p i m t", i=2),
                                         scalar1=1.0, scalar2=0.0, op0=ALU.mult, op1=ALU.add)
@@ -284,12 +279,17 @@ def tile_tinyblock_pb_t_kernel(tc, attn_bytes, attn_scale, x, wo, bo, mlp_norm_w
                 norm(s - 1)
             if in_range(s + 1, pairs):
                 x_bias(s + 1)
-            if in_range(s - 4, pairs):
-                copy_out(s - 4)
+            if in_range(s - 5, pairs):
+                copy_out(s - 5)
         last = pairs - 1
+        gelu(last - 4)
+        mx1(2 * last + 1)
         t_h(2 * last - 4)
         t_h(2 * last - 3)
+        t_out(last - 4)
+        mx2(last - 3)
         add(2 * last)
+        copy_out(last - 4)
         square(2 * last)
         add(2 * last + 1)
         norm(last, 0, 1)

@@ -67,13 +67,14 @@ def tile_tinyblock_pb_t_kernel(tc, attn_bytes, attn_scale, x, wo, bo, mlp_norm_w
         nc.vector.memset(bo_row[:], 0.0)
         nc.vector.memset(w_row[:], 0.0)
         nc.scalar.dma_start(out=sc_sb[:].rearrange("p (g t) -> p g t", g=2), in_=attn_scale.rearrange("a b (g p t) -> p (a b g) t", p=P, t=4))
-        nc.scalar.dma_start(out=w_row[0:1, :], in_=mlp_norm_w.rearrange("(a d) -> a d", a=1))
         nc.scalar.dma_start(out=b1_raw[:], in_=b1.rearrange("(p i) -> p i", i=2))
-        nc.scalar.dma_start(out=bo_row[0:1, :], in_=bo.rearrange("(a d) -> a d", a=1))
-        nc.sync.dma_start(out=a_bytes[0][:, 0:2, :], in_=bytes_view[0][:, 0:2, :])
+        nc.sync.dma_start(out=a_bytes[0][:, 0:1, :], in_=bytes_view[0][:, 0:1, :])
         nc.sync.dma_start(out=wo_raw[0][:], in_=wo_view[0])
-        nc.sync.dma_start(out=a_bytes[0][:, 2:4, :], in_=bytes_view[0][:, 2:4, :])
+        nc.sync.dma_start(out=bo_row[0:1, :], in_=bo.rearrange("(a d) -> a d", a=1))
+        nc.sync.dma_start(out=w_row[0:1, :], in_=mlp_norm_w.rearrange("(a d) -> a d", a=1))
+        nc.sync.dma_start(out=a_bytes[0][:, 1:2, :], in_=bytes_view[0][:, 1:2, :])
         nc.sync.dma_start(out=wo_raw[1][:], in_=wo_view[1])
+        nc.sync.dma_start(out=a_bytes[0][:, 2:4, :], in_=bytes_view[0][:, 2:4, :])
         nc.sync.dma_start(out=x_sb[0][:], in_=x_view[0])
         nc.sync.dma_start(out=w1_raw[:], in_=w1.rearrange("(p t) f -> p t f", t=4))
         for g in range(1, G):
@@ -117,9 +118,9 @@ def tile_tinyblock_pb_t_kernel(tc, attn_bytes, attn_scale, x, wo, bo, mlp_norm_w
             scales[m] = work.tile([P, 4 * P], U8, name="scales", align_bytes=64)
             nc.vector.quantize_mx(out=codes[m][:].bitcast(FP8X4), scales=scales[m][:], in_=grp[m][:])
 
-        def filler(i):
+        def filler(i, cols):
             psm[i] = ps2.tile([P, D], F32, name="psm")
-            nc.tensor.matmul(psm[i][:], lhsT=ones[:], rhs=bo_row[:], start=True, stop=True)
+            nc.tensor.matmul(psm[i][:, 0:cols], lhsT=ones[:], rhs=bo_row[:, 0:cols], start=True, stop=True)
 
         def mx1(i):
             m, h = divmod(i, 2)
@@ -130,10 +131,10 @@ def tile_tinyblock_pb_t_kernel(tc, attn_bytes, attn_scale, x, wo, bo, mlp_norm_w
                 nc.tensor.matmul_mx(out=psm[i][:], lhsT=codes[m][:, cols].bitcast(FP8X4), lhsT_scale=scales[m][:, cols],
                                     rhs=wo_codes[g][:].bitcast(FP8X4), rhs_scale=wo_scales[g][:], start=(g == 0), stop=(g == 1))
 
-        def x_bias(m):
+        def x_bias(m, engine=nc.gpsimd):
             g, h = divmod(m, 2)
             xbo[m] = work.tile([P, 2, D], F32, name="xbo")
-            nc.gpsimd.tensor_tensor(out=xbo[m][:], in0=x_sb[g][:, 2 * h : 2 * h + 2, :], in1=bo_sb[:].unsqueeze(1).to_broadcast([P, 2, D]), op=ALU.add)
+            engine.tensor_tensor(out=xbo[m][:], in0=x_sb[g][:, 2 * h : 2 * h + 2, :], in1=bo_sb[:].unsqueeze(1).to_broadcast([P, 2, D]), op=ALU.add)
 
         def add(i):
             if i % 2 == 0:
@@ -161,10 +162,10 @@ def tile_tinyblock_pb_t_kernel(tc, attn_bytes, attn_scale, x, wo, bo, mlp_norm_w
             hs[i] = work4.tile([P, D], BF16, name="hs")
             nc.vector.scalar_tensor_tensor(out=hs[i][:], in0=xmid[m][:, h, :], scalar=rstd[m][:, h : h + 1], in1=w_bc[:], op0=ALU.mult, op1=ALU.mult)
 
-        def t_h(i):
+        def t_h(i, pool=psh_pool, name="psh"):
             m, h = divmod(i, 2)
             if h == 0:
-                psh[m] = psh_pool.tile([P, 2, 2, P], F32, name="psh")
+                psh[m] = pool.tile([P, 2, 2, P], F32, name=name)
             words = hs[i][:].bitcast(F32)
             for u in range(2):
                 nc.tensor.transpose(psh[m][:, h, u, :], words[:, u : D // 2 : 2], ident[:])
@@ -188,7 +189,7 @@ def tile_tinyblock_pb_t_kernel(tc, attn_bytes, attn_scale, x, wo, bo, mlp_norm_w
                                     rhs=hq[m][:, P * a : P * b].bitcast(FP8X4), rhs_scale=hqs[m][:, P * a : P * b], start=True, stop=True)
 
         def gelu(m, a=0, b=2):
-            gl[m, a] = work4.tile([P, 2, P * (b - a)], F32, name="gl")
+            gl[m, a] = work6.tile([P, 2, P * (b - a)], F32, name="gl")
             for i in range(2):
                 nc.scalar.activation(out=gl[m, a][:, i, :], in_=psg[m, a][:, i, :], func=ACT.Gelu, bias=b1_sb[:, i : i + 1], scale=1.0)
 
@@ -200,7 +201,7 @@ def tile_tinyblock_pb_t_kernel(tc, attn_bytes, attn_scale, x, wo, bo, mlp_norm_w
 
         def copy_out(m, a=0, b=2, engine=nc.scalar.copy):
             g, h = divmod(m, 2)
-            og[m, a] = work4.tile([P, b - a, F], F32, name="og")
+            og[m, a] = work6.tile([P, b - a, F], F32, name="og")
             engine(out=og[m, a][:].rearrange("p j (m i) -> p j m i", i=2), in_=pso[m, a][:].rearrange("p j i m -> p j m i"))
             nc.sync.dma_start(out=out1_view[g][:, 2 * h + a : 2 * h + b, :], in_=og[m, a][:])
 
@@ -208,22 +209,25 @@ def tile_tinyblock_pb_t_kernel(tc, attn_bytes, attn_scale, x, wo, bo, mlp_norm_w
             return 0 <= i < n
 
         pairs = N_TILES // 2
+
+        def group_rows(engine, raw, grouped, lo, hi):
+            out, in_ = grouped[:, 4 * lo : 4 * hi].rearrange("p (n t) -> p n t", t=4), raw[:, :, lo:hi].rearrange("p t n -> p n t")
+            if engine == "gpsimd":
+                nc.gpsimd.tensor_scalar(out=out, in0=in_, scalar1=1.0, scalar2=0.0, op0=ALU.mult, op1=ALU.add)
+            elif engine == "scalar":
+                nc.scalar.copy(out=out, in_=in_)
+            else:
+                nc.vector.tensor_copy(out=out, in_=in_)
+
         widen(0)
         t_attn(0)
         widen(1)
         t_attn(1)
-        psb = ps2.tile([P, D], F32, name="psm")
-        nc.tensor.matmul(psb[:], lhsT=ones[:], rhs=bo_row[:], start=True, stop=True)
+        group_rows("vector", wo_raw[0], wo_grp[0], 0, D)
+        group_rows("scalar", wo_raw[1], wo_grp[1], 0, 192)
+        group_rows("gpsimd", wo_raw[1], wo_grp[1], 192, D)
         widen(2)
         widen(3)
-        nc.scalar.copy(out=bo_sb[:], in_=psb[:])
-        psw = ps2.tile([P, D], F32, name="psm")
-        nc.tensor.matmul(psw[:], lhsT=ones[:], rhs=w_row[:], start=True, stop=True)
-        nc.scalar.copy(out=w_bc[:], in_=psw[:])
-        nc.vector.tensor_copy(out=wo_grp[0][:].rearrange("p (n t) -> p n t", t=4), in_=wo_raw[0][:].rearrange("p t n -> p n t"))
-        nc.gpsimd.tensor_scalar(out=wo_grp[1][:].rearrange("p (n t) -> p n t", t=4), in0=wo_raw[1][:].rearrange("p t n -> p n t"),
-                                scalar1=1.0, scalar2=0.0, op0=ALU.mult, op1=ALU.add)
-        x_bias(0)
 
         for s in range(pairs):
             if in_range(s - 5, pairs):
@@ -236,9 +240,20 @@ def tile_tinyblock_pb_t_kernel(tc, attn_bytes, attn_scale, x, wo, bo, mlp_norm_w
                 t_attn(2 * s + 2)
             if in_range(s - 1, pairs):
                 mx1(2 * s - 1)
+            if s == 0:
+                psb = ps1.tile([P, D], F32, name="psg")
+                nc.tensor.matmul(psb[:], lhsT=ones[:], rhs=bo_row[:], start=True, stop=True)
+                nc.scalar.copy(out=bo_sb[:], in_=psb[:])
             prod(2 * s + 1)
             if in_range(s + 1, pairs):
                 t_attn(2 * s + 3)
+            if s == 0:
+                psw = ps1.tile([P, D], F32, name="pso")
+                nc.tensor.matmul(psw[:], lhsT=ones[:], rhs=w_row[:], start=True, stop=True)
+                nc.scalar.copy(out=w_bc[:], in_=psw[:])
+                x_bias(1)
+            if s == 1:
+                x_bias(0, nc.vector)
             if in_range(s - 5, pairs):
                 t_out(s - 5)
             if in_range(s - 3, pairs):
@@ -247,7 +262,7 @@ def tile_tinyblock_pb_t_kernel(tc, attn_bytes, attn_scale, x, wo, bo, mlp_norm_w
                 mx2(s - 4)
             if in_range(s - 1, pairs):
                 add(2 * s - 2)
-                filler(2 * s)
+                filler(2 * s, D)
                 add(2 * s - 1)
             if in_range(s - 3, pairs):
                 q_h(s - 3)
@@ -257,14 +272,13 @@ def tile_tinyblock_pb_t_kernel(tc, attn_bytes, attn_scale, x, wo, bo, mlp_norm_w
                     nc.vector.quantize_mx(out=wo_codes[g][:].bitcast(FP8X4), scales=wo_scales[g][:], in_=wo_grp[g][:])
             if s == 1:
                 nc.vector.tensor_copy(out=b1_sb[:], in_=b1_raw[:])
-            if s == 2:
+            if s == 3:
                 nc.vector.quantize_mx(out=w1_codes[:].bitcast(FP8X4), scales=w1_scales[:], in_=w1_grp[:])
             if in_range(s - 2, pairs):
                 gain(2 * s - 4)
                 gain(2 * s - 3)
             mx1(2 * s)
-            if s < 14:
-                filler(2 * s + 1)
+            filler(2 * s + 1, 464)
             if in_range(s + 2, pairs):
                 widen(2 * s + 4)
             if in_range(s - 1, pairs):
@@ -272,61 +286,61 @@ def tile_tinyblock_pb_t_kernel(tc, attn_bytes, attn_scale, x, wo, bo, mlp_norm_w
                 square(2 * s - 1)
             if in_range(s + 2, pairs):
                 widen(2 * s + 5)
-            if s == 1:
-                nc.gpsimd.tensor_scalar(out=w1_grp[:].rearrange("p (i m t) -> p i m t", i=2, t=4), in0=w1_raw[:].rearrange("p t (m i) -> p i m t", i=2),
-                                        scalar1=1.0, scalar2=0.0, op0=ALU.mult, op1=ALU.add)
             if in_range(s - 1, pairs):
                 norm(s - 1)
-            if in_range(s + 1, pairs):
+            if 2 <= s + 1 < pairs:
                 x_bias(s + 1)
+            if s == 2:
+                nc.gpsimd.tensor_scalar(out=w1_grp[:].rearrange("p (i m t) -> p i m t", i=2, t=4), in0=w1_raw[:].rearrange("p t (m i) -> p i m t", i=2),
+                                        scalar1=1.0, scalar2=0.0, op0=ALU.mult, op1=ALU.add)
             if in_range(s - 5, pairs):
                 copy_out(s - 5)
         last = pairs - 1
-        gelu(last - 4)
         mx1(2 * last + 1)
         t_h(2 * last - 4)
         t_h(2 * last - 3)
-        t_out(last - 4)
-        mx2(last - 3)
         add(2 * last)
-        copy_out(last - 4)
         square(2 * last)
-        add(2 * last + 1)
-        norm(last, 0, 1)
-        gelu(last - 3)
-        square(2 * last + 1)
-        h_copy(last - 2)
+        gelu(last - 4)
         gain(2 * last - 2)
+        add(2 * last + 1)
+        square(2 * last + 1)
         gain(2 * last - 1)
-        q_h(last - 2)
-        gain(2 * last)
+        mx2(last - 3)
+        h_copy(last - 2)
+        norm(last, 0, 1)
         norm(last, 1, 2)
-        t_out(last - 3)
+        t_out(last - 4)
         t_h(2 * last - 2)
         t_h(2 * last - 1)
-        mx2(last - 2)
-        h_copy(last - 1)
-        t_h(2 * last)
+        gain(2 * last)
         gain(2 * last + 1)
-        copy_out(last - 3)
-        q_h(last - 1)
+        t_h(2 * last, psa_pool, "psa")
         t_h(2 * last + 1)
-        gelu(last - 2)
+        q_h(last - 2)
+        h_copy(last - 1)
+        gelu(last - 3)
+        mx2(last - 2, 0, 2, psa_pool, "psa")
         h_copy(last, 0, 1, nc.vector.tensor_copy)
-        mx2(last - 1)
+        q_h(last - 1)
         q_h(last, 0, 1)
-        t_out(last - 2)
         h_copy(last, 1, 2, nc.vector.tensor_copy)
-        mx2(last, 0, 1, ps2, "psm")
+        mx2(last - 1, 0, 2, ps2, "psm")
+        gelu(last - 2)
+        copy_out(last - 4, 0, 2, nc.vector.tensor_copy)
+        t_out(last - 3, 0, 2, psa_pool, "psa")
         q_h(last, 1, 2)
+        mx2(last, 0, 1, ps2, "psm")
+        mx2(last, 1, 2)
         gelu(last - 1)
-        mx2(last, 1, 2, ps2, "psm")
-        copy_out(last - 2, 0, 2, nc.vector.tensor_copy)
+        t_out(last - 2, 0, 2, psa_pool, "psa")
+        copy_out(last - 3, 0, 2, nc.vector.tensor_copy)
         gelu(last, 0, 1)
         t_out(last - 1)
         gelu(last, 1, 2)
+        copy_out(last - 2, 0, 2, nc.vector.tensor_copy)
         t_out(last, 0, 1, psa_pool, "psa")
-        copy_out(last - 1, 0, 2, nc.vector.tensor_copy)
         t_out(last, 1, 2, psa_pool, "psa")
+        copy_out(last - 1, 0, 2, nc.vector.tensor_copy)
         copy_out(last, 0, 1)
-        copy_out(last, 1, 2, nc.vector.tensor_copy)
+        copy_out(last, 1, 2)

from contextlib import ExitStack

import concourse.mybir as mybir
from concourse.masks import make_identity

TOK, E, D, F = 4096, 1024, 512, 256
EPS = 1e-6
FLOPS = 2 * TOK * E * D + 2 * TOK * D * F

F32 = mybir.dt.float32
BF16 = mybir.dt.bfloat16
U32 = mybir.dt.uint32
U8 = mybir.dt.uint8
FP8 = mybir.dt.float8_e4m3fn
FP8X4 = mybir.dt.float8_e4m3fn_x4
ALU = mybir.AluOpType
ACT = mybir.ActivationFunctionType

P = 128
J = 4
G = TOK // (P * J)
N_TILES = G * J


def tile_tinyblock_pb_t_kernel(tc, attn_bytes, attn_scale, x, wo, bo, mlp_norm_w, w1, b1, out_0, out_1):
    nc = tc.nc
    bytes_view = attn_bytes.rearrange("b (g p j) k -> (b g) p j k", p=P, j=J)
    x_view = x.rearrange("b (g p j) d -> (b g) p j d", p=P, j=J)
    out0_view = out_0.rearrange("b (g p j) d -> (b g) p j d", p=P, j=J)
    out1_view = out_1.rearrange("b (g p j) f -> (b g) p j f", p=P, j=J)
    wo_view = wo.rearrange("(g p t) n -> g p t n", p=P, t=4)

    with ExitStack() as ctx:
        keep = ctx.enter_context(tc.tile_pool(name="keep", bufs=1))
        loads = ctx.enter_context(tc.tile_pool(name="loads", bufs=G))
        work = ctx.enter_context(tc.tile_pool(name="work", bufs=3))
        work6 = ctx.enter_context(tc.tile_pool(name="work6", bufs=6))
        work4 = ctx.enter_context(tc.tile_pool(name="work4", bufs=4))
        work2 = ctx.enter_context(tc.tile_pool(name="work2", bufs=2))
        ps2 = ctx.enter_context(tc.psum_pool(name="ps2", bufs=2))
        psh_pool = ctx.enter_context(tc.psum_pool(name="psh_pool", bufs=1))
        psa_pool = ctx.enter_context(tc.psum_pool(name="psa_pool", bufs=3))
        ps1 = ctx.enter_context(tc.psum_pool(name="ps1", bufs=1))
        ctx.enter_context(tc.manual_schedule())

        sc_sb = keep.tile([P, 8], F32, name="sc_sb")
        w_row = keep.tile([P, D], BF16, name="w_row")
        w_bc = keep.tile([P, D], F32, name="w_bc")
        b1_raw = keep.tile([P, 2], BF16, name="b1_raw")
        b1_sb = keep.tile([P, 2], F32, name="b1_sb")
        bo_row = keep.tile([P, D], BF16, name="bo_row")
        bo_sb = keep.tile([P, D], F32, name="bo_sb")
        ones = keep.tile([P, P], BF16, name="ones")
        ident = keep.tile([P, P], F32, name="ident")
        neg_half = keep.tile([P, 2], F32, name="neg_half")
        wo_raw = [keep.tile([P, 4, D], BF16, name="wo_raw%d" % g) for g in range(2)]
        wo_grp = [keep.tile([P, D * 4], BF16, name="wo_grp%d" % g, align_bytes=64) for g in range(2)]
        wo_codes = [keep.tile([P, D], U32, name="wo_codes%d" % g, align_bytes=64) for g in range(2)]
        wo_scales = [keep.tile([P, D], U8, name="wo_scales%d" % g, align_bytes=64) for g in range(2)]
        w1_raw = keep.tile([P, 4, F], BF16, name="w1_raw")
        w1_grp = keep.tile([P, F * 4], BF16, name="w1_grp", align_bytes=64)
        w1_codes = keep.tile([P, F], U32, name="w1_codes", align_bytes=64)
        w1_scales = keep.tile([P, F], U8, name="w1_scales", align_bytes=64)
        a_bytes = [loads.tile([P, J, E], U8, name="a_bytes") for g in range(G)]
        x_sb = [loads.tile([P, J, D], BF16, name="x_sb") for g in range(G)]

        nc.vector.memset(bo_row[:], 0.0)
        nc.vector.memset(w_row[:], 0.0)
        nc.scalar.dma_start(out=sc_sb[:].rearrange("p (g t) -> p g t", g=2), in_=attn_scale.rearrange("a b (g p t) -> p (a b g) t", p=P, t=4))
        nc.scalar.dma_start(out=b1_raw[:], in_=b1.rearrange("(p i) -> p i", i=2))
        nc.sync.dma_start(out=a_bytes[0][:, 0:1, :], in_=bytes_view[0][:, 0:1, :])
        nc.sync.dma_start(out=wo_raw[0][:], in_=wo_view[0])
        nc.sync.dma_start(out=bo_row[0:1, :], in_=bo.rearrange("(a d) -> a d", a=1))
        nc.sync.dma_start(out=w_row[0:1, :], in_=mlp_norm_w.rearrange("(a d) -> a d", a=1))
        nc.sync.dma_start(out=a_bytes[0][:, 1:2, :], in_=bytes_view[0][:, 1:2, :])
        nc.sync.dma_start(out=wo_raw[1][:], in_=wo_view[1])
        nc.sync.dma_start(out=a_bytes[0][:, 2:4, :], in_=bytes_view[0][:, 2:4, :])
        nc.sync.dma_start(out=x_sb[0][:], in_=x_view[0])
        nc.sync.dma_start(out=w1_raw[:], in_=w1.rearrange("(p t) f -> p t f", t=4))
        for g in range(1, G):
            nc.sync.dma_start(out=a_bytes[g][:], in_=bytes_view[g])
            nc.sync.dma_start(out=x_sb[g][:], in_=x_view[g])

        make_identity(nc, ident[:])
        nc.gpsimd.memset(ones[:], 1.0)
        nc.gpsimd.memset(neg_half[:], -0.5)

        wide, psa, grp, codes, scales, psm, xbo, xmid, ss, hs, psh, hgrp, hq, hqs, psg, gl, pso, og, rstd, mean = ({} for n in range(20))
        scale4 = sc_sb[:].rearrange("p (g u e) -> p g u e", g=2, u=2)

        def widen(i):
            g, j = divmod(i, J)
            wide[i] = work6.tile([P, E], BF16, name="wide")
            nc.scalar.copy(out=wide[i][:], in_=a_bytes[g][:, j, :].bitcast(FP8))

        def t_attn(i):
            psa[i] = psa_pool.tile([P, 4, P], F32, name="psa")
            words = wide[i][:].bitcast(F32)
            for g in range(2):
                for u in range(2):
                    nc.tensor.transpose(psa[i][:, 2 * g + u, :], words[:, 256 * g + u : 256 * (g + 1) : 2], ident[:])

        def prod(i):
            m, h = divmod(i, 2)
            if h == 0:
                grp[m] = work2.tile([P, 4 * 512], BF16, name="grp", align_bytes=64)
            for g in range(2):
                c0 = 512 * (2 * h + g)
                nc.vector.tensor_tensor(
                    out=grp[m][:, c0 : c0 + 512].rearrange("p (r u e) -> p r u e", u=2, e=2),
                    in0=psa[i][:, 2 * g : 2 * g + 2, :].bitcast(BF16).rearrange("p u (r e) -> p r u e", e=2),
                    in1=scale4[:, g, :, :].unsqueeze(1).to_broadcast([P, P, 2, 2]),
                    op=ALU.mult,
                )

        def q_attn(m):
            codes[m] = work.tile([P, 4 * P], U32, name="codes", align_bytes=64)
            scales[m] = work.tile([P, 4 * P], U8, name="scales", align_bytes=64)
            nc.vector.quantize_mx(out=codes[m][:].bitcast(FP8X4), scales=scales[m][:], in_=grp[m][:])

        def filler(i, cols):
            psm[i] = ps2.tile([P, D], F32, name="psm")
            nc.tensor.matmul(psm[i][:, 0:cols], lhsT=ones[:], rhs=bo_row[:, 0:cols], start=True, stop=True)

        def mx1(i):
            m, h = divmod(i, 2)
            if i not in psm:
                psm[i] = ps2.tile([P, D], F32, name="psm")
            for g in range(2):
                cols = slice(P * (2 * h + g), P * (2 * h + g + 1))
                nc.tensor.matmul_mx(out=psm[i][:], lhsT=codes[m][:, cols].bitcast(FP8X4), lhsT_scale=scales[m][:, cols],
                                    rhs=wo_codes[g][:].bitcast(FP8X4), rhs_scale=wo_scales[g][:], start=(g == 0), stop=(g == 1))

        def x_bias(m, engine=nc.gpsimd):
            g, h = divmod(m, 2)
            xbo[m] = work.tile([P, 2, D], F32, name="xbo")
            engine.tensor_tensor(out=xbo[m][:], in0=x_sb[g][:, 2 * h : 2 * h + 2, :], in1=bo_sb[:].unsqueeze(1).to_broadcast([P, 2, D]), op=ALU.add)

        def add(i):
            if i % 2 == 0:
                xmid[i // 2] = work4.tile([P, 2, D], F32, name="xmid")
            nc.vector.tensor_tensor(out=xmid[i // 2][:, i % 2, :], in0=psm[i][:], in1=xbo[i // 2][:, i % 2, :], op=ALU.add)
            if i % 2 == 1:
                g, j = divmod(i, J)
                nc.sync.dma_start(out=out0_view[g][:, j - 1 : j + 1, :], in_=xmid[i // 2][:])

        def square(i):
            junk = work2.tile([P, D], BF16, name="junk")
            if i % 2 == 0:
                ss[i // 2] = work4.tile([P, 2], F32, name="ss")
            nc.scalar.activation(out=junk[:], in_=xmid[i // 2][:, i % 2, :], func=ACT.Square, accum_out=ss[i // 2][:, i % 2 : i % 2 + 1])

        def norm(m, a=0, b=2):
            if a == 0:
                rstd[m] = work4.tile([P, 2], F32, name="rstd")
                mean[m] = work4.tile([P, 2], F32, name="mean")
            nc.vector.tensor_scalar(out=mean[m][:, a:b], in0=ss[m][:, a:b], scalar1=1.0 / D, scalar2=EPS, op0=ALU.mult, op1=ALU.add)
            nc.gpsimd.tensor_tensor(out=rstd[m][:, a:b], in0=mean[m][:, a:b], in1=neg_half[:, a:b], op=ALU.pow)

        def gain(i):
            m, h = divmod(i, 2)
            hs[i] = work4.tile([P, D], BF16, name="hs")
            nc.vector.scalar_tensor_tensor(out=hs[i][:], in0=xmid[m][:, h, :], scalar=rstd[m][:, h : h + 1], in1=w_bc[:], op0=ALU.mult, op1=ALU.mult)

        def t_h(i, pool=psh_pool, name="psh"):
            m, h = divmod(i, 2)
            if h == 0:
                psh[m] = pool.tile([P, 2, 2, P], F32, name=name)
            words = hs[i][:].bitcast(F32)
            for u in range(2):
                nc.tensor.transpose(psh[m][:, h, u, :], words[:, u : D // 2 : 2], ident[:])

        def h_copy(m, a=0, b=2, engine=nc.scalar.copy):
            if a == 0:
                hgrp[m] = work2.tile([P, 2 * D], BF16, name="hgrp", align_bytes=64)
            engine(out=hgrp[m][:, D * a : D * b].bitcast(F32).rearrange("p (h r u) -> p h r u", h=b - a, u=2), in_=psh[m][:, a:b, :, :].rearrange("p h u r -> p h r u"))

        def q_h(m, a=0, b=2):
            if a == 0:
                hq[m] = work2.tile([P, 2 * P], U32, name="hq", align_bytes=64)
                hqs[m] = work2.tile([P, 2 * P], U8, name="hqs", align_bytes=64)
            nc.vector.quantize_mx(out=hq[m][:, P * a : P * b].bitcast(FP8X4), scales=hqs[m][:, P * a : P * b], in_=hgrp[m][:, D * a : D * b])

        def mx2(m, a=0, b=2, pool=ps1, name="psg"):
            psg[m, a] = pool.tile([P, 2, P * (b - a)], F32, name=name)
            for i in range(2):
                cols = slice(P * i, P * (i + 1))
                nc.tensor.matmul_mx(out=psg[m, a][:, i, :], lhsT=w1_codes[:, cols].bitcast(FP8X4), lhsT_scale=w1_scales[:, cols],
                                    rhs=hq[m][:, P * a : P * b].bitcast(FP8X4), rhs_scale=hqs[m][:, P * a : P * b], start=True, stop=True)

        def gelu(m, a=0, b=2):
            gl[m, a] = work6.tile([P, 2, P * (b - a)], F32, name="gl")
            for i in range(2):
                nc.scalar.activation(out=gl[m, a][:, i, :], in_=psg[m, a][:, i, :], func=ACT.Gelu, bias=b1_sb[:, i : i + 1], scale=1.0)

        def t_out(m, a=0, b=2, pool=ps1, name="pso"):
            pso[m, a] = pool.tile([P, b - a, 2, P], F32, name=name)
            for j in range(b - a):
                for i in range(2):
                    nc.tensor.transpose(pso[m, a][:, j, i, :], gl[m, a][:, i, P * j : P * (j + 1)], ident[:])

        def copy_out(m, a=0, b=2, engine=nc.scalar.copy):
            g, h = divmod(m, 2)
            og[m, a] = work6.tile([P, b - a, F], F32, name="og")
            engine(out=og[m, a][:].rearrange("p j (m i) -> p j m i", i=2), in_=pso[m, a][:].rearrange("p j i m -> p j m i"))
            nc.sync.dma_start(out=out1_view[g][:, 2 * h + a : 2 * h + b, :], in_=og[m, a][:])

        def in_range(i, n=N_TILES):
            return 0 <= i < n

        pairs = N_TILES // 2

        def group_rows(engine, raw, grouped, lo, hi):
            out, in_ = grouped[:, 4 * lo : 4 * hi].rearrange("p (n t) -> p n t", t=4), raw[:, :, lo:hi].rearrange("p t n -> p n t")
            if engine == "gpsimd":
                nc.gpsimd.tensor_scalar(out=out, in0=in_, scalar1=1.0, scalar2=0.0, op0=ALU.mult, op1=ALU.add)
            elif engine == "scalar":
                nc.scalar.copy(out=out, in_=in_)
            else:
                nc.vector.tensor_copy(out=out, in_=in_)

        widen(0)
        t_attn(0)
        widen(1)
        t_attn(1)
        group_rows("vector", wo_raw[0], wo_grp[0], 0, D)
        group_rows("scalar", wo_raw[1], wo_grp[1], 0, 192)
        group_rows("gpsimd", wo_raw[1], wo_grp[1], 192, D)
        widen(2)
        widen(3)

        for s in range(pairs):
            if in_range(s - 5, pairs):
                gelu(s - 5)
            prod(2 * s)
            if in_range(s - 3, pairs):
                t_h(2 * s - 6)
                t_h(2 * s - 5)
            if in_range(s + 1, pairs):
                t_attn(2 * s + 2)
            if in_range(s - 1, pairs):
                mx1(2 * s - 1)
            if s == 0:
                psb = ps1.tile([P, D], F32, name="psg")
                nc.tensor.matmul(psb[:], lhsT=ones[:], rhs=bo_row[:], start=True, stop=True)
                nc.scalar.copy(out=bo_sb[:], in_=psb[:])
            prod(2 * s + 1)
            if in_range(s + 1, pairs):
                t_attn(2 * s + 3)
            if s == 0:
                psw = ps1.tile([P, D], F32, name="pso")
                nc.tensor.matmul(psw[:], lhsT=ones[:], rhs=w_row[:], start=True, stop=True)
                nc.scalar.copy(out=w_bc[:], in_=psw[:])
                x_bias(1)
            if s == 1:
                x_bias(0, nc.vector)
            if in_range(s - 5, pairs):
                t_out(s - 5)
            if in_range(s - 3, pairs):
                h_copy(s - 3)
            if in_range(s - 4, pairs):
                mx2(s - 4)
            if in_range(s - 1, pairs):
                add(2 * s - 2)
                filler(2 * s, D)
                add(2 * s - 1)
            if in_range(s - 3, pairs):
                q_h(s - 3)
            q_attn(s)
            if s == 0:
                for g in (0, 1):
                    nc.vector.quantize_mx(out=wo_codes[g][:].bitcast(FP8X4), scales=wo_scales[g][:], in_=wo_grp[g][:])
            if s == 1:
                nc.vector.tensor_copy(out=b1_sb[:], in_=b1_raw[:])
            if s == 3:
                nc.vector.quantize_mx(out=w1_codes[:].bitcast(FP8X4), scales=w1_scales[:], in_=w1_grp[:])
            if in_range(s - 2, pairs):
                gain(2 * s - 4)
                gain(2 * s - 3)
            mx1(2 * s)
            filler(2 * s + 1, 464)
            if in_range(s + 2, pairs):
                widen(2 * s + 4)
            if in_range(s - 1, pairs):
                square(2 * s - 2)
                square(2 * s - 1)
            if in_range(s + 2, pairs):
                widen(2 * s + 5)
            if in_range(s - 1, pairs):
                norm(s - 1)
            if 2 <= s + 1 < pairs:
                x_bias(s + 1)
            if s == 2:
                nc.gpsimd.tensor_scalar(out=w1_grp[:].rearrange("p (i m t) -> p i m t", i=2, t=4), in0=w1_raw[:].rearrange("p t (m i) -> p i m t", i=2),
                                        scalar1=1.0, scalar2=0.0, op0=ALU.mult, op1=ALU.add)
            if in_range(s - 5, pairs):
                copy_out(s - 5)
        last = pairs - 1
        mx1(2 * last + 1)
        t_h(2 * last - 4)
        t_h(2 * last - 3)
        add(2 * last)
        square(2 * last)
        gelu(last - 4)
        gain(2 * last - 2)
        add(2 * last + 1)
        square(2 * last + 1)
        gain(2 * last - 1)
        mx2(last - 3)
        h_copy(last - 2)
        norm(last, 0, 1)
        norm(last, 1, 2)
        t_out(last - 4)
        t_h(2 * last - 2)
        t_h(2 * last - 1)
        gain(2 * last)
        gain(2 * last + 1)
        t_h(2 * last, psa_pool, "psa")
        t_h(2 * last + 1)
        q_h(last - 2)
        h_copy(last - 1)
        gelu(last - 3)
        mx2(last - 2, 0, 2, psa_pool, "psa")
        h_copy(last, 0, 1, nc.vector.tensor_copy)
        q_h(last - 1)
        q_h(last, 0, 1)
        h_copy(last, 1, 2, nc.vector.tensor_copy)
        mx2(last - 1, 0, 2, ps2, "psm")
        gelu(last - 2)
        copy_out(last - 4, 0, 2, nc.vector.tensor_copy)
        t_out(last - 3, 0, 2, psa_pool, "psa")
        q_h(last, 1, 2)
        mx2(last, 0, 1, ps2, "psm")
        mx2(last, 1, 2)
        gelu(last - 1)
        t_out(last - 2, 0, 2, psa_pool, "psa")
        copy_out(last - 3, 0, 2, nc.vector.tensor_copy)
        gelu(last, 0, 1)
        t_out(last - 1)
        gelu(last, 1, 2)
        copy_out(last - 2, 0, 2, nc.vector.tensor_copy)
        t_out(last, 0, 1, psa_pool, "psa")
        t_out(last, 1, 2, psa_pool, "psa")
        copy_out(last - 1, 0, 2, nc.vector.tensor_copy)
        copy_out(last, 0, 1)
        copy_out(last, 1, 2)
